import numpy as np
import ml_dtypes


def mxq(x, axis, fmt="e4m3"):
    dtype, down = {"e4m3": (ml_dtypes.float8_e4m3fn, 7), "e5m2": (ml_dtypes.float8_e5m2, 14)}[fmt]
    v = np.moveaxis(np.asarray(x, np.float32).astype(ml_dtypes.bfloat16).astype(np.float64), axis, -1)
    blocks = v.reshape(v.shape[:-1] + (-1, 32))
    amax = np.abs(blocks).max(-1, keepdims=True)
    byte = np.maximum(np.where(amax > 0, np.frexp(amax)[1] - 1 + 127, 0) - down, 1)
    scale = np.exp2(byte - 127.0)
    codes = (blocks / scale).astype(np.float32).astype(dtype).astype(np.float64)
    return np.moveaxis((codes * scale).reshape(v.shape), -1, axis)


WIDE = False


def mx_kscale(k):
    if not WIDE:
        return np.ones(k)
    levels = np.array([10, -10, 5, -5, 0])
    a = np.random.permutation(np.resize(levels, k // 512 * 4)).reshape(k // 512, 4)
    idx = np.arange(k)
    return np.exp2(a[idx // 512, idx % 128 // 32])


BF16 = ml_dtypes.bfloat16


def bf(x):
    return np.asarray(x, np.float32).astype(BF16)


def f64(x):
    return np.asarray(x).astype(np.float64)


B, L, E, H, C, EO = 2, 2048, 128, 1, 1024, 2048
HD = E // H
G = L // C
NH = B * H


def setup_inputs():
    t = mx_kscale(C)
    return {"q_chunks": bf(np.random.standard_normal((NH, G, C, HD)) / np.sqrt(HD)),
            "k_chunks": bf(np.random.standard_normal((NH, G, C, HD)) * 0.5 * t[:, None]),
            "v_chunks": bf(np.random.standard_normal((NH, G, C, HD)) * 6.0 / np.sqrt(C) / t[:, None])}


def reference(q_chunks, k_chunks, v_chunks):
    logits = f64(q_chunks) @ f64(k_chunks).transpose(0, 1, 3, 2)
    p = np.maximum(logits, 0.0)
    return mxq(p, 3, "e4m3") @ mxq(f64(v_chunks), 2, "e4m3")

@@ -1,0 +1,189 @@
+from contextlib import ExitStack
+
+import concourse.mybir as mybir
+from concourse.masks import make_identity
+
+BF16 = mybir.dt.bfloat16
+F32 = mybir.dt.float32
+U32 = mybir.dt.uint32
+U8 = mybir.dt.uint8
+FP8X4 = mybir.dt.float8_e4m3fn_x4
+RELU = mybir.ActivationFunctionType.Relu
+
+P = 128
+PACK = 4
+SLICES = 4
+CHUNK = 1024
+HEAD = 128
+PASSES = CHUNK // (P * PACK)
+Q_TILES = CHUNK // P
+Q_GROUP = 4
+GROUPS = Q_TILES // Q_GROUP
+UNITS = SLICES * GROUPS * PASSES
+UNITS_PER_SLICE = GROUPS * PASSES
+WORK_BANKS = 6
+
+FLOPS = 2 * 2 * SLICES * CHUNK * CHUNK * HEAD
+
+
+def tile_normlocalattention_pa_t_kernel(tc, q_chunks, k_chunks, v_chunks, out):
+    nc = tc.nc
+
+    q_dram = q_chunks.rearrange("n g (p t) d -> (n g) p t d", t=Q_TILES)
+    k_dram = k_chunks.rearrange("n g (c p j) d -> (n g) p c j d", c=PASSES, j=PACK)
+    v_dram = v_chunks.rearrange("n g (c p j) d -> (n g) p c j d", c=PASSES, j=PACK)
+    out_dram = out.rearrange("n g (p t) d -> (n g) p t d", t=Q_TILES)
+
+    with ExitStack() as ctx:
+        const = ctx.enter_context(tc.tile_pool(name="const", bufs=1))
+        per_slice = ctx.enter_context(tc.tile_pool(name="per_slice", bufs=SLICES))
+        per_unit = ctx.enter_context(tc.tile_pool(name="per_unit", bufs=6))
+        work_banks = ctx.enter_context(tc.psum_pool(name="work_banks", bufs=WORK_BANKS))
+        out_banks = ctx.enter_context(tc.psum_pool(name="out_banks", bufs=2))
+
+        identity = const.tile([P, P], BF16)
+        make_identity(nc, identity[:])
+
+        k_in, q_in, v_in = [], [], []
+        for s in range(SLICES):
+            k_rows = per_slice.tile([P, PASSES, PACK, HEAD], BF16)
+            nc.sync.dma_start(out=k_rows[:], in_=k_dram[s, :, :, :, :])
+            q_rows = per_slice.tile([P, Q_TILES, HEAD], BF16)
+            nc.sync.dma_start(out=q_rows[:], in_=q_dram[s, :, :, :])
+            v_rows = per_slice.tile([P, PASSES, PACK, HEAD], BF16)
+            nc.sync.dma_start(out=v_rows[:], in_=v_dram[s, :, :, :, :])
+            k_in.append(k_rows)
+            q_in.append(q_rows)
+            v_in.append(v_rows)
+
+        k_t, q_t, v_grouped, v_codes, v_scales = [], [], [], [], []
+        for s in range(SLICES):
+            k_cols = per_slice.tile([P, PASSES, PACK, P], BF16)
+            q_cols = per_slice.tile([P, Q_TILES, P], BF16)
+            v_quads = per_slice.tile([P, PASSES, HEAD, PACK], BF16, align_bytes=64)
+            v_words = per_slice.tile([P, PASSES, HEAD], U32, align_bytes=64)
+            v_plane = per_slice.tile([P, PASSES, HEAD], U8, align_bytes=64)
+            k_t.append(k_cols)
+            q_t.append(q_cols)
+            v_grouped.append(v_quads)
+            v_codes.append(v_words)
+            v_scales.append(v_plane)
+
+        def transpose_four(s, piece):
+            half = piece // 2
+            t_bank = work_banks.tile([P, 4, P], BF16, tag="bank")
+            if piece % 2 == 0:
+                rows, cols = k_in[s][:, half, :, :], k_t[s][:, half, :, :]
+            else:
+                tiles = slice(half * Q_GROUP, (half + 1) * Q_GROUP)
+                rows, cols = q_in[s][:, tiles, :], q_t[s][:, tiles, :]
+            for i in range(4):
+                nc.tensor.transpose(out=t_bank[:, i, :], in_=rows[:, i, :], identity=identity[:])
+            if piece % 2 == 0:
+                nc.vector.tensor_copy(out=cols, in_=t_bank[:])
+            else:
+                nc.scalar.copy(out=cols, in_=t_bank[:])
+
+        def regroup_values(s, c):
+            nc.vector.tensor_copy(
+                out=v_grouped[s][:, c, :, :],
+                in_=v_in[s][:, c, :, :].rearrange("p j d -> p d j"),
+            )
+
+        def quantise_values(s, c):
+            nc.vector.quantize_mx(
+                out=v_codes[s][:, c, :].bitcast(FP8X4),
+                scales=v_scales[s][:, c, :],
+                in_=v_grouped[s][:, c, :, :].rearrange("p d j -> p (d j)"),
+            )
+
+        p_grouped, p_codes, p_scales = {}, {}, {}
+
+        def score_bank(u, i):
+            s, c = u // UNITS_PER_SLICE, u % PASSES
+            t = (u // PASSES) % GROUPS * Q_GROUP + i
+            s_bank = work_banks.tile([P, PACK, P], F32, tag="bank")
+            for j in range(PACK):
+                nc.tensor.matmul(
+                    out=s_bank[:, j, :],
+                    lhsT=k_t[s][:, c, j, :],
+                    rhs=q_t[s][:, t, :],
+                    start=True,
+                    stop=True,
+                )
+            by_query = s_bank[:].rearrange("p j q -> p q j")
+            if i == 0:
+                nc.vector.tensor_scalar_max(out=p_grouped[u][:, i, :, :], in0=by_query, scalar1=0.0)
+            else:
+                nc.scalar.activation(out=p_grouped[u][:, i, :, :], in_=by_query, func=RELU)
+
+        def quantise_scores(u):
+            nc.vector.quantize_mx(
+                out=p_codes[u][:].bitcast(FP8X4),
+                scales=p_scales[u][:],
+                in_=p_grouped[u][:].rearrange("p i q j -> p (i q j)"),
+            )
+
+        o_banks = {}
+
+        def attend(g):
+            s = g // GROUPS
+            o_bank = out_banks.tile([P, Q_GROUP, HEAD], F32)
+            o_banks[g] = o_bank
+            for i in range(Q_GROUP):
+                queries = slice(i * P, (i + 1) * P)
+                for c in range(PASSES):
+                    u = g * PASSES + c
+                    nc.tensor.matmul_mx(
+                        out=o_bank[:, i, :],
+                        lhsT=p_codes[u][:, queries].bitcast(FP8X4),
+                        lhsT_scale=p_scales[u][:, queries],
+                        rhs=v_codes[s][:, c, :].bitcast(FP8X4),
+                        rhs_scale=v_scales[s][:, c, :],
+                        start=(c == 0),
+                        stop=(c == PASSES - 1),
+                    )
+
+        def store(g):
+            s = g // GROUPS
+            tiles = slice(g % GROUPS * Q_GROUP, (g % GROUPS + 1) * Q_GROUP)
+            o_rows = per_unit.tile([P, Q_GROUP, HEAD], F32)
+            nc.vector.tensor_copy(out=o_rows[:], in_=o_banks[g][:])
+            nc.sync.dma_start(out=out_dram[s, :, tiles, :], in_=o_rows[:])
+
+        for piece in range(UNITS_PER_SLICE):
+            transpose_four(0, piece)
+        for c in range(PASSES):
+            regroup_values(0, c)
+        for c in range(PASSES):
+            quantise_values(0, c)
+
+        for u in range(UNITS):
+            upcoming = u // UNITS_PER_SLICE + 1
+            piece = u % UNITS_PER_SLICE
+            prepare = upcoming < SLICES
+            quads = per_unit.tile([P, Q_GROUP, P, PACK], BF16, align_bytes=64)
+            words = per_unit.tile([P, Q_GROUP * P], U32, align_bytes=64)
+            plane = per_unit.tile([P, Q_GROUP * P], U8, align_bytes=64)
+            p_grouped[u], p_codes[u], p_scales[u] = quads, words, plane
+
+            score_bank(u, 0)
+            if prepare and piece % 2 == 0:
+                regroup_values(upcoming, piece // 2)
+            if u >= 1:
+                quantise_scores(u - 1)
+            score_bank(u, 1)
+            if prepare:
+                transpose_four(upcoming, piece)
+            score_bank(u, 2)
+            score_bank(u, 3)
+            if prepare and piece % 2 == 0:
+                quantise_values(upcoming, piece // 2)
+            if u % PASSES == 0 and u >= PASSES:
+                attend(u // PASSES - 1)
+            if u % PASSES == 1 and u >= PASSES:
+                store(u // PASSES - 1)
+
+        quantise_scores(UNITS - 1)
+        attend(UNITS // PASSES - 1)
+        store(UNITS // PASSES - 1)

@@ -40,6 +40,7 @@ def tile_normlocalattention_pa_t_kernel(tc, q_chunks, k_chunks, v_chunks, out):
         per_unit = ctx.enter_context(tc.tile_pool(name="per_unit", bufs=6))
         work_banks = ctx.enter_context(tc.psum_pool(name="work_banks", bufs=WORK_BANKS))
         out_banks = ctx.enter_context(tc.psum_pool(name="out_banks", bufs=2))
+        ctx.enter_context(tc.manual_schedule())
 
         identity = const.tile([P, P], BF16)
         make_identity(nc, identity[:])

@@ -19,8 +19,13 @@ PASSES = CHUNK // (P * PACK)
 Q_TILES = CHUNK // P
 Q_GROUP = 4
 GROUPS = Q_TILES // Q_GROUP
-UNITS = SLICES * GROUPS * PASSES
 UNITS_PER_SLICE = GROUPS * PASSES
+UNITS = SLICES * UNITS_PER_SLICE
+PIECES_PER_SLICE = PASSES + GROUPS
+PIECES = SLICES * PIECES_PER_SLICE
+PIECES_AHEAD = 3
+ATTEND_LAG = 2
+STORE_LAG = 3
 WORK_BANKS = 6
 
 FLOPS = 2 * 2 * SLICES * CHUNK * CHUNK * HEAD
@@ -48,10 +53,12 @@ def tile_normlocalattention_pa_t_kernel(tc, q_chunks, k_chunks, v_chunks, out):
         k_in, q_in, v_in = [], [], []
         for s in range(SLICES):
             k_rows = per_slice.tile([P, PASSES, PACK, HEAD], BF16)
-            nc.sync.dma_start(out=k_rows[:], in_=k_dram[s, :, :, :, :])
             q_rows = per_slice.tile([P, Q_TILES, HEAD], BF16)
-            nc.sync.dma_start(out=q_rows[:], in_=q_dram[s, :, :, :])
             v_rows = per_slice.tile([P, PASSES, PACK, HEAD], BF16)
+            for half in range(2):
+                tiles = slice(half * Q_GROUP, (half + 1) * Q_GROUP)
+                nc.sync.dma_start(out=k_rows[:, half, :, :], in_=k_dram[s, :, half, :, :])
+                nc.sync.dma_start(out=q_rows[:, tiles, :], in_=q_dram[s, :, tiles, :])
             nc.sync.dma_start(out=v_rows[:], in_=v_dram[s, :, :, :, :])
             k_in.append(k_rows)
             q_in.append(q_rows)
@@ -70,25 +77,25 @@ def tile_normlocalattention_pa_t_kernel(tc, q_chunks, k_chunks, v_chunks, out):
             v_codes.append(v_words)
             v_scales.append(v_plane)
 
-        def transpose_four(s, piece):
-            half = piece // 2
+        def transpose_piece(m):
+            s, half, is_k = m // PIECES_PER_SLICE, m % PIECES_PER_SLICE // 2, m % 2 == 0
             t_bank = work_banks.tile([P, 4, P], BF16, tag="bank")
-            if piece % 2 == 0:
+            if is_k:
                 rows, cols = k_in[s][:, half, :, :], k_t[s][:, half, :, :]
             else:
                 tiles = slice(half * Q_GROUP, (half + 1) * Q_GROUP)
                 rows, cols = q_in[s][:, tiles, :], q_t[s][:, tiles, :]
             for i in range(4):
                 nc.tensor.transpose(out=t_bank[:, i, :], in_=rows[:, i, :], identity=identity[:])
-            if piece % 2 == 0:
+            if is_k:
                 nc.vector.tensor_copy(out=cols, in_=t_bank[:])
             else:
                 nc.scalar.copy(out=cols, in_=t_bank[:])
 
         def regroup_values(s, c):
             nc.vector.tensor_copy(
-                out=v_grouped[s][:, c, :, :],
-                in_=v_in[s][:, c, :, :].rearrange("p j d -> p d j"),
+                out=v_grouped[s][:, c, :, :].rearrange("p (a i) j -> p a j i", i=4),
+                in_=v_in[s][:, c, :, :].rearrange("p j (a i) -> p a j i", i=4),
             )
 
         def quantise_values(s, c):
@@ -152,39 +159,33 @@ def tile_normlocalattention_pa_t_kernel(tc, q_chunks, k_chunks, v_chunks, out):
             nc.vector.tensor_copy(out=o_rows[:], in_=o_banks[g][:])
             nc.sync.dma_start(out=out_dram[s, :, tiles, :], in_=o_rows[:])
 
-        for piece in range(UNITS_PER_SLICE):
-            transpose_four(0, piece)
-        for c in range(PASSES):
-            regroup_values(0, c)
-        for c in range(PASSES):
-            quantise_values(0, c)
+        for m in range(PIECES_AHEAD):
+            transpose_piece(m)
 
-        for u in range(UNITS):
-            upcoming = u // UNITS_PER_SLICE + 1
-            piece = u % UNITS_PER_SLICE
-            prepare = upcoming < SLICES
-            quads = per_unit.tile([P, Q_GROUP, P, PACK], BF16, align_bytes=64)
-            words = per_unit.tile([P, Q_GROUP * P], U32, align_bytes=64)
-            plane = per_unit.tile([P, Q_GROUP * P], U8, align_bytes=64)
-            p_grouped[u], p_codes[u], p_scales[u] = quads, words, plane
-
-            score_bank(u, 0)
-            if prepare and piece % 2 == 0:
-                regroup_values(upcoming, piece // 2)
-            if u >= 1:
+        for u in range(UNITS + STORE_LAG):
+            scoring = u < UNITS
+            values = scoring and u % 2 == 0
+            s, c = u // UNITS_PER_SLICE, u % UNITS_PER_SLICE // 2
+            if scoring:
+                quads = per_unit.tile([P, Q_GROUP, P, PACK], BF16, align_bytes=64)
+                words = per_unit.tile([P, Q_GROUP * P], U32, align_bytes=64)
+                plane = per_unit.tile([P, Q_GROUP * P], U8, align_bytes=64)
+                p_grouped[u], p_codes[u], p_scales[u] = quads, words, plane
+                score_bank(u, 0)
+            if values:
+                regroup_values(s, c)
+            if 1 <= u <= UNITS:
                 quantise_scores(u - 1)
-            score_bank(u, 1)
-            if prepare:
-                transpose_four(upcoming, piece)
-            score_bank(u, 2)
-            score_bank(u, 3)
-            if prepare and piece % 2 == 0:
-                quantise_values(upcoming, piece // 2)
-            if u % PASSES == 0 and u >= PASSES:
-                attend(u // PASSES - 1)
-            if u % PASSES == 1 and u >= PASSES:
-                store(u // PASSES - 1)
-
-        quantise_scores(UNITS - 1)
-        attend(UNITS // PASSES - 1)
-        store(UNITS // PASSES - 1)
+            if scoring:
+                score_bank(u, 1)
+            if u + PIECES_AHEAD < PIECES:
+                transpose_piece(u + PIECES_AHEAD)
+            if scoring:
+                score_bank(u, 2)
+                score_bank(u, 3)
+            if values:
+                quantise_values(s, c)
+            if (u - ATTEND_LAG) % PASSES == 1 and u >= ATTEND_LAG:
+                attend((u - ATTEND_LAG) // PASSES)
+            if (u - STORE_LAG) % PASSES == 1 and u >= STORE_LAG:
+                store((u - STORE_LAG) // PASSES)

@@ -17,18 +17,32 @@ CHUNK = 1024
 HEAD = 128
 PASSES = CHUNK // (P * PACK)
 Q_TILES = CHUNK // P
-Q_GROUP = 4
+BANKS = SLICES * Q_TILES * PASSES
+
+Q_GROUP = 2
 GROUPS = Q_TILES // Q_GROUP
-UNITS_PER_SLICE = GROUPS * PASSES
-UNITS = SLICES * UNITS_PER_SLICE
-PIECES_PER_SLICE = PASSES + GROUPS
+GROUP_BANKS = Q_GROUP * PASSES
+
+PIECE = 4
+PIECES_PER_SLICE = (PASSES * PACK + Q_TILES) // PIECE
 PIECES = SLICES * PIECES_PER_SLICE
+BANKS_PER_PIECE = BANKS // PIECES
 PIECES_AHEAD = 3
-ATTEND_LAG = 2
-STORE_LAG = 3
+V_PASSES = SLICES * PASSES
+BANKS_PER_V_PASS = BANKS // V_PASSES
+
+VECTOR_EVERY = 4
 WORK_BANKS = 6
+ATTEND_LAG = 8
+STORE_LAG = 10
 
 FLOPS = 2 * 2 * SLICES * CHUNK * CHUNK * HEAD
+
+
+def group_ending_at(n):
+    if 0 <= n < BANKS and (n + 1) % GROUP_BANKS == 0:
+        return n // GROUP_BANKS
+    return None
 
 
 def tile_normlocalattention_pa_t_kernel(tc, q_chunks, k_chunks, v_chunks, out):
@@ -42,7 +56,7 @@ def tile_normlocalattention_pa_t_kernel(tc, q_chunks, k_chunks, v_chunks, out):
     with ExitStack() as ctx:
         const = ctx.enter_context(tc.tile_pool(name="const", bufs=1))
         per_slice = ctx.enter_context(tc.tile_pool(name="per_slice", bufs=SLICES))
-        per_unit = ctx.enter_context(tc.tile_pool(name="per_unit", bufs=6))
+        per_unit = ctx.enter_context(tc.tile_pool(name="per_unit", bufs=8))
         work_banks = ctx.enter_context(tc.psum_pool(name="work_banks", bufs=WORK_BANKS))
         out_banks = ctx.enter_context(tc.psum_pool(name="out_banks", bufs=2))
         ctx.enter_context(tc.manual_schedule())
@@ -56,10 +70,11 @@ def tile_normlocalattention_pa_t_kernel(tc, q_chunks, k_chunks, v_chunks, out):
             q_rows = per_slice.tile([P, Q_TILES, HEAD], BF16)
             v_rows = per_slice.tile([P, PASSES, PACK, HEAD], BF16)
             for half in range(2):
-                tiles = slice(half * Q_GROUP, (half + 1) * Q_GROUP)
+                tiles = slice(half * PIECE, (half + 1) * PIECE)
                 nc.sync.dma_start(out=k_rows[:, half, :, :], in_=k_dram[s, :, half, :, :])
                 nc.sync.dma_start(out=q_rows[:, tiles, :], in_=q_dram[s, :, tiles, :])
-            nc.sync.dma_start(out=v_rows[:], in_=v_dram[s, :, :, :, :])
+                if half == 0:
+                    nc.sync.dma_start(out=v_rows[:], in_=v_dram[s, :, :, :, :])
             k_in.append(k_rows)
             q_in.append(q_rows)
             v_in.append(v_rows)
@@ -79,26 +94,28 @@ def tile_normlocalattention_pa_t_kernel(tc, q_chunks, k_chunks, v_chunks, out):
 
         def transpose_piece(m):
             s, half, is_k = m // PIECES_PER_SLICE, m % PIECES_PER_SLICE // 2, m % 2 == 0
-            t_bank = work_banks.tile([P, 4, P], BF16, tag="bank")
+            t_bank = work_banks.tile([P, PIECE, P], BF16, tag="bank")
             if is_k:
                 rows, cols = k_in[s][:, half, :, :], k_t[s][:, half, :, :]
             else:
-                tiles = slice(half * Q_GROUP, (half + 1) * Q_GROUP)
+                tiles = slice(half * PIECE, (half + 1) * PIECE)
                 rows, cols = q_in[s][:, tiles, :], q_t[s][:, tiles, :]
-            for i in range(4):
+            for i in range(PIECE):
                 nc.tensor.transpose(out=t_bank[:, i, :], in_=rows[:, i, :], identity=identity[:])
             if is_k:
                 nc.vector.tensor_copy(out=cols, in_=t_bank[:])
             else:
                 nc.scalar.copy(out=cols, in_=t_bank[:])
 
-        def regroup_values(s, c):
+        def regroup_values(w):
+            s, c = w // PASSES, w % PASSES
             nc.vector.tensor_copy(
                 out=v_grouped[s][:, c, :, :].rearrange("p (a i) j -> p a j i", i=4),
                 in_=v_in[s][:, c, :, :].rearrange("p j (a i) -> p a j i", i=4),
             )
 
-        def quantise_values(s, c):
+        def quantise_values(w):
+            s, c = w // PASSES, w % PASSES
             nc.vector.quantize_mx(
                 out=v_codes[s][:, c, :].bitcast(FP8X4),
                 scales=v_scales[s][:, c, :],
@@ -107,9 +124,15 @@ def tile_normlocalattention_pa_t_kernel(tc, q_chunks, k_chunks, v_chunks, out):
 
         p_grouped, p_codes, p_scales = {}, {}, {}
 
-        def score_bank(u, i):
-            s, c = u // UNITS_PER_SLICE, u % PASSES
-            t = (u // PASSES) % GROUPS * Q_GROUP + i
+        def score_bank(n):
+            u, i = n // Q_GROUP, n % Q_GROUP
+            g, c = u // PASSES, u % PASSES
+            s, t = g // GROUPS, g % GROUPS * Q_GROUP + i
+            if i == 0:
+                quads = per_unit.tile([P, Q_GROUP, P, PACK], BF16, align_bytes=64)
+                words = per_unit.tile([P, Q_GROUP * P], U32, align_bytes=64)
+                plane = per_unit.tile([P, Q_GROUP * P], U8, align_bytes=64)
+                p_grouped[u], p_codes[u], p_scales[u] = quads, words, plane
             s_bank = work_banks.tile([P, PACK, P], F32, tag="bank")
             for j in range(PACK):
                 nc.tensor.matmul(
@@ -120,7 +143,7 @@ def tile_normlocalattention_pa_t_kernel(tc, q_chunks, k_chunks, v_chunks, out):
                     stop=True,
                 )
             by_query = s_bank[:].rearrange("p j q -> p q j")
-            if i == 0:
+            if n % VECTOR_EVERY == 0:
                 nc.vector.tensor_scalar_max(out=p_grouped[u][:, i, :, :], in0=by_query, scalar1=0.0)
             else:
                 nc.scalar.activation(out=p_grouped[u][:, i, :, :], in_=by_query, func=RELU)
@@ -159,33 +182,28 @@ def tile_normlocalattention_pa_t_kernel(tc, q_chunks, k_chunks, v_chunks, out):
             nc.vector.tensor_copy(out=o_rows[:], in_=o_banks[g][:])
             nc.sync.dma_start(out=out_dram[s, :, tiles, :], in_=o_rows[:])
 
-        for m in range(PIECES_AHEAD):
-            transpose_piece(m)
+        transpose_piece(0)
+        transpose_piece(1)
+        regroup_values(0)
+        transpose_piece(2)
+        quantise_values(0)
 
-        for u in range(UNITS + STORE_LAG):
-            scoring = u < UNITS
-            values = scoring and u % 2 == 0
-            s, c = u // UNITS_PER_SLICE, u % UNITS_PER_SLICE // 2
-            if scoring:
-                quads = per_unit.tile([P, Q_GROUP, P, PACK], BF16, align_bytes=64)
-                words = per_unit.tile([P, Q_GROUP * P], U32, align_bytes=64)
-                plane = per_unit.tile([P, Q_GROUP * P], U8, align_bytes=64)
-                p_grouped[u], p_codes[u], p_scales[u] = quads, words, plane
-                score_bank(u, 0)
-            if values:
-                regroup_values(s, c)
-            if 1 <= u <= UNITS:
-                quantise_scores(u - 1)
-            if scoring:
-                score_bank(u, 1)
-            if u + PIECES_AHEAD < PIECES:
-                transpose_piece(u + PIECES_AHEAD)
-            if scoring:
-                score_bank(u, 2)
-                score_bank(u, 3)
-            if values:
-                quantise_values(s, c)
-            if (u - ATTEND_LAG) % PASSES == 1 and u >= ATTEND_LAG:
-                attend((u - ATTEND_LAG) // PASSES)
-            if (u - STORE_LAG) % PASSES == 1 and u >= STORE_LAG:
-                store((u - STORE_LAG) // PASSES)
+        for n in range(BANKS + STORE_LAG):
+            if n < BANKS:
+                score_bank(n)
+            w = n // BANKS_PER_V_PASS + 1
+            if n % BANKS_PER_V_PASS == 0 and w < V_PASSES:
+                regroup_values(w)
+            if n % Q_GROUP == 0 and 0 < n <= BANKS:
+                quantise_scores(n // Q_GROUP - 1)
+            m = n // BANKS_PER_PIECE + PIECES_AHEAD
+            if n % BANKS_PER_PIECE == 1 and m < PIECES:
+                transpose_piece(m)
+            if n % BANKS_PER_V_PASS == 3 and w < V_PASSES:
+                quantise_values(w)
+            g = group_ending_at(n - ATTEND_LAG)
+            if g is not None:
+                attend(g)
+            g = group_ending_at(n - STORE_LAG)
+            if g is not None:
+                store(g)

@@ -18,31 +18,25 @@ HEAD = 128
 PASSES = CHUNK // (P * PACK)
 Q_TILES = CHUNK // P
 BANKS = SLICES * Q_TILES * PASSES
+SLICE_BANKS = Q_TILES * PASSES
+HALF = 4
 
-Q_GROUP = 2
-GROUPS = Q_TILES // Q_GROUP
-GROUP_BANKS = Q_GROUP * PASSES
-
-PIECE = 4
-PIECES_PER_SLICE = (PASSES * PACK + Q_TILES) // PIECE
-PIECES = SLICES * PIECES_PER_SLICE
-BANKS_PER_PIECE = BANKS // PIECES
-PIECES_AHEAD = 3
-V_PASSES = SLICES * PASSES
-BANKS_PER_V_PASS = BANKS // V_PASSES
-
-VECTOR_EVERY = 4
+SLICE_GROUPS = ((4, 4), (4, 4), (4, 4), (4, 2, 2))
+MAX_GROUP = 4
 WORK_BANKS = 6
-ATTEND_LAG = 8
-STORE_LAG = 10
+OUT_BANKS = 2
+QUANT_LAG = 2
+ATTEND_LAG = 10
+STORE_LAG = 12
+K_AT, Q_AT, REGROUP_AT, VQUANT_AT = [6, 10, 8, 12]
+VECTOR_BANKS = [0]
+VECTOR_PERIOD = 5
+SCALAR_STORES = 3
+K_COPY_ON_VECTOR = True
+Q_COPY_ON_VECTOR = True
+WARM = 0
 
 FLOPS = 2 * 2 * SLICES * CHUNK * CHUNK * HEAD
-
-
-def group_ending_at(n):
-    if 0 <= n < BANKS and (n + 1) % GROUP_BANKS == 0:
-        return n // GROUP_BANKS
-    return None
 
 
 def tile_normlocalattention_pa_t_kernel(tc, q_chunks, k_chunks, v_chunks, out):
@@ -53,12 +47,29 @@ def tile_normlocalattention_pa_t_kernel(tc, q_chunks, k_chunks, v_chunks, out):
     v_dram = v_chunks.rearrange("n g (c p j) d -> (n g) p c j d", c=PASSES, j=PACK)
     out_dram = out.rearrange("n g (p t) d -> (n g) p t d", t=Q_TILES)
 
+    groups, units, banks = [], [], []
+    unit_end, group_end = {}, {}
+    for s in range(SLICES):
+        first = 0
+        for size in SLICE_GROUPS[s]:
+            g = len(groups)
+            groups.append((s, first, size))
+            first += size
+            for c in range(PASSES):
+                u = len(units)
+                units.append((g, c))
+                for i in range(size):
+                    banks.append((u, i))
+                unit_end[len(banks) - 1] = u
+            group_end[len(banks) - 1] = g
+    assert len(banks) == BANKS
+
     with ExitStack() as ctx:
         const = ctx.enter_context(tc.tile_pool(name="const", bufs=1))
         per_slice = ctx.enter_context(tc.tile_pool(name="per_slice", bufs=SLICES))
         per_unit = ctx.enter_context(tc.tile_pool(name="per_unit", bufs=8))
         work_banks = ctx.enter_context(tc.psum_pool(name="work_banks", bufs=WORK_BANKS))
-        out_banks = ctx.enter_context(tc.psum_pool(name="out_banks", bufs=2))
+        out_banks = ctx.enter_context(tc.psum_pool(name="out_banks", bufs=OUT_BANKS))
         ctx.enter_context(tc.manual_schedule())
 
         identity = const.tile([P, P], BF16)
@@ -69,19 +80,23 @@ def tile_normlocalattention_pa_t_kernel(tc, q_chunks, k_chunks, v_chunks, out):
             k_rows = per_slice.tile([P, PASSES, PACK, HEAD], BF16)
             q_rows = per_slice.tile([P, Q_TILES, HEAD], BF16)
             v_rows = per_slice.tile([P, PASSES, PACK, HEAD], BF16)
-            for half in range(2):
-                tiles = slice(half * PIECE, (half + 1) * PIECE)
-                nc.sync.dma_start(out=k_rows[:, half, :, :], in_=k_dram[s, :, half, :, :])
-                nc.sync.dma_start(out=q_rows[:, tiles, :], in_=q_dram[s, :, tiles, :])
-                if half == 0:
-                    nc.sync.dma_start(out=v_rows[:], in_=v_dram[s, :, :, :, :])
+            if s == 0:
+                nc.sync.dma_start(out=k_rows[:, 0, :, :], in_=k_dram[s, :, 0, :, :])
+                nc.sync.dma_start(out=q_rows[:, 0:HALF, :], in_=q_dram[s, :, 0:HALF, :])
+                nc.sync.dma_start(out=k_rows[:, 1, :, :], in_=k_dram[s, :, 1, :, :])
+                nc.sync.dma_start(out=v_rows[:], in_=v_dram[s, :, :, :, :])
+                nc.sync.dma_start(out=q_rows[:, HALF:Q_TILES, :], in_=q_dram[s, :, HALF:Q_TILES, :])
+            else:
+                nc.sync.dma_start(out=k_rows[:], in_=k_dram[s, :, :, :, :])
+                nc.sync.dma_start(out=q_rows[:], in_=q_dram[s, :, :, :])
+                nc.sync.dma_start(out=v_rows[:], in_=v_dram[s, :, :, :, :])
             k_in.append(k_rows)
             q_in.append(q_rows)
             v_in.append(v_rows)
 
         k_t, q_t, v_grouped, v_codes, v_scales = [], [], [], [], []
         for s in range(SLICES):
-            k_cols = per_slice.tile([P, PASSES, PACK, P], BF16)
+            k_cols = per_slice.tile([P, PASSES * PACK, P], BF16)
             q_cols = per_slice.tile([P, Q_TILES, P], BF16)
             v_quads = per_slice.tile([P, PASSES, HEAD, PACK], BF16, align_bytes=64)
             v_words = per_slice.tile([P, PASSES, HEAD], U32, align_bytes=64)
@@ -92,76 +107,75 @@ def tile_normlocalattention_pa_t_kernel(tc, q_chunks, k_chunks, v_chunks, out):
             v_codes.append(v_words)
             v_scales.append(v_plane)
 
-        def transpose_piece(m):
-            s, half, is_k = m // PIECES_PER_SLICE, m % PIECES_PER_SLICE // 2, m % 2 == 0
-            t_bank = work_banks.tile([P, PIECE, P], BF16, tag="bank")
+        def transpose_piece(is_k, s, lo, hi, on_vector):
+            t_bank = work_banks.tile([P, hi - lo, P], BF16, tag="bank")
             if is_k:
-                rows, cols = k_in[s][:, half, :, :], k_t[s][:, half, :, :]
+                rows, cols = k_in[s][:].rearrange("p c j d -> p (c j) d"), k_t[s]
             else:
-                tiles = slice(half * PIECE, (half + 1) * PIECE)
-                rows, cols = q_in[s][:, tiles, :], q_t[s][:, tiles, :]
-            for i in range(PIECE):
-                nc.tensor.transpose(out=t_bank[:, i, :], in_=rows[:, i, :], identity=identity[:])
-            if is_k:
-                nc.vector.tensor_copy(out=cols, in_=t_bank[:])
+                rows, cols = q_in[s][:], q_t[s]
+            for i in range(lo, hi):
+                nc.tensor.transpose(out=t_bank[:, i - lo, :], in_=rows[:, i, :], identity=identity[:])
+            if on_vector:
+                nc.vector.tensor_copy(out=cols[:, lo:hi, :], in_=t_bank[:])
             else:
-                nc.scalar.copy(out=cols, in_=t_bank[:])
+                nc.scalar.copy(out=cols[:, lo:hi, :], in_=t_bank[:])
 
-        def regroup_values(w):
-            s, c = w // PASSES, w % PASSES
-            nc.vector.tensor_copy(
-                out=v_grouped[s][:, c, :, :].rearrange("p (a i) j -> p a j i", i=4),
-                in_=v_in[s][:, c, :, :].rearrange("p j (a i) -> p a j i", i=4),
-            )
+        def regroup_values(s):
+            for c in range(PASSES):
+                nc.vector.tensor_copy(
+                    out=v_grouped[s][:, c, :, :].rearrange("p (a i) j -> p a j i", i=4),
+                    in_=v_in[s][:, c, :, :].rearrange("p j (a i) -> p a j i", i=4),
+                )
 
-        def quantise_values(w):
-            s, c = w // PASSES, w % PASSES
+        def quantise_values(s):
             nc.vector.quantize_mx(
-                out=v_codes[s][:, c, :].bitcast(FP8X4),
-                scales=v_scales[s][:, c, :],
-                in_=v_grouped[s][:, c, :, :].rearrange("p d j -> p (d j)"),
+                out=v_codes[s][:].rearrange("p c d -> p (c d)").bitcast(FP8X4),
+                scales=v_scales[s][:].rearrange("p c d -> p (c d)"),
+                in_=v_grouped[s][:].rearrange("p c d j -> p (c d j)"),
             )
 
         p_grouped, p_codes, p_scales = {}, {}, {}
 
         def score_bank(n):
-            u, i = n // Q_GROUP, n % Q_GROUP
-            g, c = u // PASSES, u % PASSES
-            s, t = g // GROUPS, g % GROUPS * Q_GROUP + i
+            u, i = banks[n]
+            g, c = units[u]
+            s, first, size = groups[g]
+            t = first + i
             if i == 0:
-                quads = per_unit.tile([P, Q_GROUP, P, PACK], BF16, align_bytes=64)
-                words = per_unit.tile([P, Q_GROUP * P], U32, align_bytes=64)
-                plane = per_unit.tile([P, Q_GROUP * P], U8, align_bytes=64)
+                quads = per_unit.tile([P, MAX_GROUP, P, PACK], BF16, align_bytes=64)
+                words = per_unit.tile([P, MAX_GROUP * P], U32, align_bytes=64)
+                plane = per_unit.tile([P, MAX_GROUP * P], U8, align_bytes=64)
                 p_grouped[u], p_codes[u], p_scales[u] = quads, words, plane
             s_bank = work_banks.tile([P, PACK, P], F32, tag="bank")
             for j in range(PACK):
                 nc.tensor.matmul(
                     out=s_bank[:, j, :],
-                    lhsT=k_t[s][:, c, j, :],
+                    lhsT=k_t[s][:, c * PACK + j, :],
                     rhs=q_t[s][:, t, :],
                     start=True,
                     stop=True,
                 )
             by_query = s_bank[:].rearrange("p j q -> p q j")
-            if n % VECTOR_EVERY == 0:
+            if n % VECTOR_PERIOD in VECTOR_BANKS:
                 nc.vector.tensor_scalar_max(out=p_grouped[u][:, i, :, :], in0=by_query, scalar1=0.0)
             else:
                 nc.scalar.activation(out=p_grouped[u][:, i, :, :], in_=by_query, func=RELU)
 
         def quantise_scores(u):
+            size = groups[units[u][0]][2]
             nc.vector.quantize_mx(
-                out=p_codes[u][:].bitcast(FP8X4),
-                scales=p_scales[u][:],
-                in_=p_grouped[u][:].rearrange("p i q j -> p (i q j)"),
+                out=p_codes[u][:, 0 : size * P].bitcast(FP8X4),
+                scales=p_scales[u][:, 0 : size * P],
+                in_=p_grouped[u][:, 0:size, :, :].rearrange("p i q j -> p (i q j)"),
             )
 
         o_banks = {}
 
         def attend(g):
-            s = g // GROUPS
-            o_bank = out_banks.tile([P, Q_GROUP, HEAD], F32)
+            s, first, size = groups[g]
+            o_bank = out_banks.tile([P, MAX_GROUP, HEAD], F32)
             o_banks[g] = o_bank
-            for i in range(Q_GROUP):
+            for i in range(size):
                 queries = slice(i * P, (i + 1) * P)
                 for c in range(PASSES):
                     u = g * PASSES + c
@@ -176,34 +190,40 @@ def tile_normlocalattention_pa_t_kernel(tc, q_chunks, k_chunks, v_chunks, out):
                     )
 
         def store(g):
-            s = g // GROUPS
-            tiles = slice(g % GROUPS * Q_GROUP, (g % GROUPS + 1) * Q_GROUP)
-            o_rows = per_unit.tile([P, Q_GROUP, HEAD], F32)
-            nc.vector.tensor_copy(out=o_rows[:], in_=o_banks[g][:])
-            nc.sync.dma_start(out=out_dram[s, :, tiles, :], in_=o_rows[:])
+            s, first, size = groups[g]
+            o_rows = per_unit.tile([P, MAX_GROUP, HEAD], F32)
+            if g >= len(groups) - SCALAR_STORES:
+                nc.scalar.copy(out=o_rows[:, 0:size, :], in_=o_banks[g][:, 0:size, :])
+            else:
+                nc.vector.tensor_copy(out=o_rows[:, 0:size, :], in_=o_banks[g][:, 0:size, :])
+            nc.sync.dma_start(out=out_dram[s, :, first : first + size, :], in_=o_rows[:, 0:size, :])
 
-        transpose_piece(0)
-        transpose_piece(1)
-        regroup_values(0)
-        transpose_piece(2)
-        quantise_values(0)
+        transpose_piece(True, 0, 0, HALF, True)
+        transpose_piece(False, 0, 0, HALF, False)
 
-        for n in range(BANKS + STORE_LAG):
+        for n in range(BANKS + STORE_LAG + 1):
             if n < BANKS:
                 score_bank(n)
-            w = n // BANKS_PER_V_PASS + 1
-            if n % BANKS_PER_V_PASS == 0 and w < V_PASSES:
-                regroup_values(w)
-            if n % Q_GROUP == 0 and 0 < n <= BANKS:
-                quantise_scores(n // Q_GROUP - 1)
-            m = n // BANKS_PER_PIECE + PIECES_AHEAD
-            if n % BANKS_PER_PIECE == 1 and m < PIECES:
-                transpose_piece(m)
-            if n % BANKS_PER_V_PASS == 3 and w < V_PASSES:
-                quantise_values(w)
-            g = group_ending_at(n - ATTEND_LAG)
-            if g is not None:
-                attend(g)
-            g = group_ending_at(n - STORE_LAG)
-            if g is not None:
-                store(g)
+            if n == 1:
+                transpose_piece(True, 0, HALF, 2 * HALF, True)
+            if n == 2:
+                regroup_values(0)
+            if n == 4:
+                transpose_piece(False, 0, HALF, 2 * HALF, False)
+                quantise_values(0)
+            if n - QUANT_LAG in unit_end:
+                quantise_scores(unit_end[n - QUANT_LAG])
+            s, r = n // SLICE_BANKS + 1, n % SLICE_BANKS
+            if s < SLICES:
+                if r == K_AT:
+                    transpose_piece(True, s, 0, 2 * HALF, K_COPY_ON_VECTOR)
+                if r == Q_AT:
+                    transpose_piece(False, s, 0, 2 * HALF, Q_COPY_ON_VECTOR)
+                if r == REGROUP_AT:
+                    regroup_values(s)
+                if r == VQUANT_AT:
+                    quantise_values(s)
+            if n - ATTEND_LAG in group_end:
+                attend(group_end[n - ATTEND_LAG])
+            if n - STORE_LAG in group_end:
+                store(group_end[n - STORE_LAG])

@@ -30,11 +30,12 @@ ATTEND_LAG = 10
 STORE_LAG = 12
 K_AT, Q_AT, REGROUP_AT, VQUANT_AT = [6, 10, 8, 12]
 VECTOR_BANKS = [0]
-VECTOR_PERIOD = 5
+VECTOR_PERIOD = 4
 SCALAR_STORES = 3
 K_COPY_ON_VECTOR = True
 Q_COPY_ON_VECTOR = True
 WARM = 0
+REGROUP_ON_GPSIMD = True
 
 FLOPS = 2 * 2 * SLICES * CHUNK * CHUNK * HEAD
 
@@ -122,6 +123,16 @@ def tile_normlocalattention_pa_t_kernel(tc, q_chunks, k_chunks, v_chunks, out):
 
         def regroup_values(s):
             for c in range(PASSES):
+                if REGROUP_ON_GPSIMD:
+                    nc.gpsimd.tensor_scalar(
+                        out=v_grouped[s][:, c, :, :],
+                        in0=v_in[s][:, c, :, :].rearrange("p j d -> p d j"),
+                        scalar1=1.0,
+                        scalar2=0.0,
+                        op0=mybir.AluOpType.mult,
+                        op1=mybir.AluOpType.add,
+                    )
+                    continue
                 nc.vector.tensor_copy(
                     out=v_grouped[s][:, c, :, :].rearrange("p (a i) j -> p a j i", i=4),
                     in_=v_in[s][:, c, :, :].rearrange("p j (a i) -> p a j i", i=4),

@@ -35,6 +35,11 @@ SCALAR_STORES = 3
 K_COPY_ON_VECTOR = True
 Q_COPY_ON_VECTOR = True
 WARM = 0
+PACED = True
+PACE_EVERY, PACE_AT = (8, 2)
+V_BUFS = 1
+EXTRA_AT = ()
+SHARE = 1
 REGROUP_ON_GPSIMD = True
 
 FLOPS = 2 * 2 * SLICES * CHUNK * CHUNK * HEAD
@@ -69,6 +74,7 @@ def tile_normlocalattention_pa_t_kernel(tc, q_chunks, k_chunks, v_chunks, out):
         const = ctx.enter_context(tc.tile_pool(name="const", bufs=1))
         per_slice = ctx.enter_context(tc.tile_pool(name="per_slice", bufs=SLICES))
         per_unit = ctx.enter_context(tc.tile_pool(name="per_unit", bufs=8))
+        one_pass = ctx.enter_context(tc.tile_pool(name="one_pass", bufs=V_BUFS))
         work_banks = ctx.enter_context(tc.psum_pool(name="work_banks", bufs=WORK_BANKS))
         out_banks = ctx.enter_context(tc.psum_pool(name="out_banks", bufs=OUT_BANKS))
         ctx.enter_context(tc.manual_schedule())
@@ -145,7 +151,31 @@ def tile_normlocalattention_pa_t_kernel(tc, q_chunks, k_chunks, v_chunks, out):
                 in_=v_grouped[s][:].rearrange("p c d j -> p (c d j)"),
             )
 
+        v_pass = {}
+
+        def regroup_pass(w):
+            s, c = w // PASSES, w % PASSES
+            quads_v = one_pass.tile([P, HEAD, PACK], BF16, align_bytes=64)
+            v_pass[w] = quads_v
+            nc.gpsimd.tensor_scalar(
+                out=quads_v[:],
+                in0=v_in[s][:, c, :, :].rearrange("p j d -> p d j"),
+                scalar1=1.0,
+                scalar2=0.0,
+                op0=mybir.AluOpType.mult,
+                op1=mybir.AluOpType.add,
+            )
+
+        def quantise_pass(w):
+            s, c = w // PASSES, w % PASSES
+            nc.vector.quantize_mx(
+                out=v_codes[s][:, c, :].bitcast(FP8X4),
+                scales=v_scales[s][:, c, :],
+                in_=v_pass[w][:].rearrange("p d j -> p (d j)"),
+            )
+
         p_grouped, p_codes, p_scales = {}, {}, {}
+        s_banks = {}
 
         def score_bank(n):
             u, i = banks[n]
@@ -157,16 +187,28 @@ def tile_normlocalattention_pa_t_kernel(tc, q_chunks, k_chunks, v_chunks, out):
                 words = per_unit.tile([P, MAX_GROUP * P], U32, align_bytes=64)
                 plane = per_unit.tile([P, MAX_GROUP * P], U8, align_bytes=64)
                 p_grouped[u], p_codes[u], p_scales[u] = quads, words, plane
-            s_bank = work_banks.tile([P, PACK, P], F32, tag="bank")
-            for j in range(PACK):
-                nc.tensor.matmul(
-                    out=s_bank[:, j, :],
-                    lhsT=k_t[s][:, c * PACK + j, :],
-                    rhs=q_t[s][:, t, :],
-                    start=True,
-                    stop=True,
-                )
-            by_query = s_bank[:].rearrange("p j q -> p q j")
+            if i % SHARE == 0:
+                for e in range(SHARE):
+                    s_bank = work_banks.tile([P, PACK, P], F32, tag="bank")
+                    s_banks[n + e] = s_bank
+                if n % 8 in EXTRA_AT:
+                    nc.tensor.matmul(
+                        out=s_banks[n][:, 0, :],
+                        lhsT=k_t[s][:, c * PACK, :],
+                        rhs=q_t[s][:, t, :],
+                        start=True,
+                        stop=True,
+                    )
+                for j in range(PACK):
+                    for e in range(SHARE):
+                        nc.tensor.matmul(
+                            out=s_banks[n + e][:, j, :],
+                            lhsT=k_t[s][:, c * PACK + j, :],
+                            rhs=q_t[s][:, t + e, :],
+                            start=True,
+                            stop=True,
+                        )
+            by_query = s_banks[n][:].rearrange("p j q -> p q j")
             if n % VECTOR_PERIOD in VECTOR_BANKS:
                 nc.vector.tensor_scalar_max(out=p_grouped[u][:, i, :, :], in0=by_query, scalar1=0.0)
             else:
@@ -209,6 +251,8 @@ def tile_normlocalattention_pa_t_kernel(tc, q_chunks, k_chunks, v_chunks, out):
                 nc.vector.tensor_copy(out=o_rows[:, 0:size, :], in_=o_banks[g][:, 0:size, :])
             nc.sync.dma_start(out=out_dram[s, :, first : first + size, :], in_=o_rows[:, 0:size, :])
 
+        if PACED:
+            regroup_pass(0)
         transpose_piece(True, 0, 0, HALF, True)
         transpose_piece(False, 0, 0, HALF, False)
 
@@ -217,22 +261,27 @@ def tile_normlocalattention_pa_t_kernel(tc, q_chunks, k_chunks, v_chunks, out):
                 score_bank(n)
             if n == 1:
                 transpose_piece(True, 0, HALF, 2 * HALF, True)
-            if n == 2:
+            if n == 2 and not PACED:
                 regroup_values(0)
             if n == 4:
                 transpose_piece(False, 0, HALF, 2 * HALF, False)
-                quantise_values(0)
+                if not PACED:
+                    quantise_values(0)
             if n - QUANT_LAG in unit_end:
                 quantise_scores(unit_end[n - QUANT_LAG])
             s, r = n // SLICE_BANKS + 1, n % SLICE_BANKS
+            if PACED and n % PACE_EVERY == PACE_AT and n // PACE_EVERY < SLICES * PASSES:
+                quantise_pass(n // PACE_EVERY)
+                if n // PACE_EVERY + 1 < SLICES * PASSES:
+                    regroup_pass(n // PACE_EVERY + 1)
             if s < SLICES:
                 if r == K_AT:
                     transpose_piece(True, s, 0, 2 * HALF, K_COPY_ON_VECTOR)
                 if r == Q_AT:
                     transpose_piece(False, s, 0, 2 * HALF, Q_COPY_ON_VECTOR)
-                if r == REGROUP_AT:
+                if r == REGROUP_AT and not PACED:
                     regroup_values(s)
-                if r == VQUANT_AT:
+                if r == VQUANT_AT and not PACED:
                     quantise_values(s)
             if n - ATTEND_LAG in group_end:
                 attend(group_end[n - ATTEND_LAG])

@@ -34,7 +34,8 @@ VECTOR_PERIOD = 4
 SCALAR_STORES = 3
 K_COPY_ON_VECTOR = True
 Q_COPY_ON_VECTOR = True
-WARM = 0
+WARM = 3
+HEAD_SPLIT = True
 PACED = True
 PACE_EVERY, PACE_AT = (8, 2)
 V_BUFS = 1
@@ -87,7 +88,14 @@ def tile_normlocalattention_pa_t_kernel(tc, q_chunks, k_chunks, v_chunks, out):
             k_rows = per_slice.tile([P, PASSES, PACK, HEAD], BF16)
             q_rows = per_slice.tile([P, Q_TILES, HEAD], BF16)
             v_rows = per_slice.tile([P, PASSES, PACK, HEAD], BF16)
-            if s == 0:
+            if s == 0 and HEAD_SPLIT:
+                nc.sync.dma_start(out=q_rows[:, 0:2, :], in_=q_dram[s, :, 0:2, :])
+                nc.sync.dma_start(out=k_rows[:, 0, :, :], in_=k_dram[s, :, 0, :, :])
+                nc.sync.dma_start(out=q_rows[:, 2:HALF, :], in_=q_dram[s, :, 2:HALF, :])
+                nc.sync.dma_start(out=k_rows[:, 1, :, :], in_=k_dram[s, :, 1, :, :])
+                nc.sync.dma_start(out=v_rows[:], in_=v_dram[s, :, :, :, :])
+                nc.sync.dma_start(out=q_rows[:, HALF:Q_TILES, :], in_=q_dram[s, :, HALF:Q_TILES, :])
+            elif s == 0:
                 nc.sync.dma_start(out=k_rows[:, 0, :, :], in_=k_dram[s, :, 0, :, :])
                 nc.sync.dma_start(out=q_rows[:, 0:HALF, :], in_=q_dram[s, :, 0:HALF, :])
                 nc.sync.dma_start(out=k_rows[:, 1, :, :], in_=k_dram[s, :, 1, :, :])
@@ -251,20 +259,35 @@ def tile_normlocalattention_pa_t_kernel(tc, q_chunks, k_chunks, v_chunks, out):
                 nc.vector.tensor_copy(out=o_rows[:, 0:size, :], in_=o_banks[g][:, 0:size, :])
             nc.sync.dma_start(out=out_dram[s, :, first : first + size, :], in_=o_rows[:, 0:size, :])
 
+        if WARM:
+            zeros = const.tile([P, 4 * P], BF16)
+            nc.vector.memset(zeros[:], 0.0)
+            w_bank = work_banks.tile([P, 4 * P], F32, tag="bank")
+            for i in range(WARM):
+                nc.tensor.matmul(out=w_bank[:], lhsT=zeros[:, 0:P], rhs=zeros[:], start=True, stop=True)
         if PACED:
             regroup_pass(0)
-        transpose_piece(True, 0, 0, HALF, True)
-        transpose_piece(False, 0, 0, HALF, False)
+        if HEAD_SPLIT:
+            transpose_piece(False, 0, 0, 2, True)
+            transpose_piece(True, 0, 0, HALF, True)
+            transpose_piece(False, 0, 2, HALF, False)
+            transpose_piece(True, 0, HALF, 2 * HALF, True)
+        else:
+            transpose_piece(True, 0, 0, HALF, True)
+            transpose_piece(False, 0, 0, HALF, False)
 
         for n in range(BANKS + STORE_LAG + 1):
             if n < BANKS:
                 score_bank(n)
-            if n == 1:
+            if n == 1 and not HEAD_SPLIT:
                 transpose_piece(True, 0, HALF, 2 * HALF, True)
+            if n == 3 and HEAD_SPLIT:
+                transpose_piece(False, 0, HALF, 2 * HALF, True)
             if n == 2 and not PACED:
                 regroup_values(0)
             if n == 4:
-                transpose_piece(False, 0, HALF, 2 * HALF, False)
+                if not HEAD_SPLIT:
+                    transpose_piece(False, 0, HALF, 2 * HALF, False)
                 if not PACED:
                     quantise_values(0)
             if n - QUANT_LAG in unit_end:

@@ -23,11 +23,11 @@ HALF = 4
 
 SLICE_GROUPS = ((4, 4), (4, 4), (4, 4), (4, 2, 2))
 MAX_GROUP = 4
-WORK_BANKS = 6
-OUT_BANKS = 2
-QUANT_LAG = 2
-ATTEND_LAG = 10
-STORE_LAG = 12
+WORK_BANKS = 7
+OUT_BANKS = 1
+QUANT_LAG = 3
+ATTEND_LAG = 12
+STORE_LAG = 14
 K_AT, Q_AT, REGROUP_AT, VQUANT_AT = [6, 10, 8, 12]
 VECTOR_BANKS = [0]
 VECTOR_PERIOD = 4
@@ -35,6 +35,15 @@ SCALAR_STORES = 3
 K_COPY_ON_VECTOR = True
 Q_COPY_ON_VECTOR = True
 WARM = 3
+SCALAR_QUEUE = False
+EXTRA_VECTOR = ()
+V0_LAST = False
+Q47_AT = 3
+VQ0_AT = 2
+TAIL_WORK = 3
+FOUR_AT = ()
+TWO_QUEUES = False
+WARM_EARLY = False
 HEAD_SPLIT = True
 PACED = True
 PACE_EVERY, PACE_AT = (8, 2)
@@ -80,6 +89,13 @@ def tile_normlocalattention_pa_t_kernel(tc, q_chunks, k_chunks, v_chunks, out):
         out_banks = ctx.enter_context(tc.psum_pool(name="out_banks", bufs=OUT_BANKS))
         ctx.enter_context(tc.manual_schedule())
 
+        if WARM and WARM_EARLY:
+            zeros = const.tile([P, P], BF16)
+            nc.gpsimd.memset(zeros[:], 0.0)
+            w_bank = work_banks.tile([P, P], F32, tag="bank")
+            for i in range(WARM):
+                nc.tensor.matmul(out=w_bank[:], lhsT=zeros[:], rhs=zeros[:], start=True, stop=True)
+
         identity = const.tile([P, P], BF16)
         make_identity(nc, identity[:])
 
@@ -89,12 +105,17 @@ def tile_normlocalattention_pa_t_kernel(tc, q_chunks, k_chunks, v_chunks, out):
             q_rows = per_slice.tile([P, Q_TILES, HEAD], BF16)
             v_rows = per_slice.tile([P, PASSES, PACK, HEAD], BF16)
             if s == 0 and HEAD_SPLIT:
-                nc.sync.dma_start(out=q_rows[:, 0:2, :], in_=q_dram[s, :, 0:2, :])
+                second = nc.scalar if TWO_QUEUES else nc.sync
+                second.dma_start(out=q_rows[:, 0:2, :], in_=q_dram[s, :, 0:2, :])
                 nc.sync.dma_start(out=k_rows[:, 0, :, :], in_=k_dram[s, :, 0, :, :])
-                nc.sync.dma_start(out=q_rows[:, 2:HALF, :], in_=q_dram[s, :, 2:HALF, :])
+                second.dma_start(out=q_rows[:, 2:HALF, :], in_=q_dram[s, :, 2:HALF, :])
                 nc.sync.dma_start(out=k_rows[:, 1, :, :], in_=k_dram[s, :, 1, :, :])
-                nc.sync.dma_start(out=v_rows[:], in_=v_dram[s, :, :, :, :])
-                nc.sync.dma_start(out=q_rows[:, HALF:Q_TILES, :], in_=q_dram[s, :, HALF:Q_TILES, :])
+                if V0_LAST:
+                    nc.sync.dma_start(out=q_rows[:, HALF:Q_TILES, :], in_=q_dram[s, :, HALF:Q_TILES, :])
+                    nc.sync.dma_start(out=v_rows[:], in_=v_dram[s, :, :, :, :])
+                else:
+                    nc.sync.dma_start(out=v_rows[:], in_=v_dram[s, :, :, :, :])
+                    nc.sync.dma_start(out=q_rows[:, HALF:Q_TILES, :], in_=q_dram[s, :, HALF:Q_TILES, :])
             elif s == 0:
                 nc.sync.dma_start(out=k_rows[:, 0, :, :], in_=k_dram[s, :, 0, :, :])
                 nc.sync.dma_start(out=q_rows[:, 0:HALF, :], in_=q_dram[s, :, 0:HALF, :])
@@ -217,7 +238,7 @@ def tile_normlocalattention_pa_t_kernel(tc, q_chunks, k_chunks, v_chunks, out):
                             stop=True,
                         )
             by_query = s_banks[n][:].rearrange("p j q -> p q j")
-            if n % VECTOR_PERIOD in VECTOR_BANKS:
+            if n % VECTOR_PERIOD in VECTOR_BANKS or n in EXTRA_VECTOR:
                 nc.vector.tensor_scalar_max(out=p_grouped[u][:, i, :, :], in0=by_query, scalar1=0.0)
             else:
                 nc.scalar.activation(out=p_grouped[u][:, i, :, :], in_=by_query, func=RELU)
@@ -234,7 +255,10 @@ def tile_normlocalattention_pa_t_kernel(tc, q_chunks, k_chunks, v_chunks, out):
 
         def attend(g):
             s, first, size = groups[g]
-            o_bank = out_banks.tile([P, MAX_GROUP, HEAD], F32)
+            if g >= len(groups) - TAIL_WORK:
+                o_bank = work_banks.tile([P, MAX_GROUP, HEAD], F32, tag="bank")
+            else:
+                o_bank = out_banks.tile([P, MAX_GROUP, HEAD], F32, tag="out")
             o_banks[g] = o_bank
             for i in range(size):
                 queries = slice(i * P, (i + 1) * P)
@@ -257,9 +281,12 @@ def tile_normlocalattention_pa_t_kernel(tc, q_chunks, k_chunks, v_chunks, out):
                 nc.scalar.copy(out=o_rows[:, 0:size, :], in_=o_banks[g][:, 0:size, :])
             else:
                 nc.vector.tensor_copy(out=o_rows[:, 0:size, :], in_=o_banks[g][:, 0:size, :])
-            nc.sync.dma_start(out=out_dram[s, :, first : first + size, :], in_=o_rows[:, 0:size, :])
+            if g >= len(groups) - SCALAR_STORES and SCALAR_QUEUE:
+                nc.scalar.dma_start(out=out_dram[s, :, first : first + size, :], in_=o_rows[:, 0:size, :])
+            else:
+                nc.sync.dma_start(out=out_dram[s, :, first : first + size, :], in_=o_rows[:, 0:size, :])
 
-        if WARM:
+        if WARM and not WARM_EARLY:
             zeros = const.tile([P, 4 * P], BF16)
             nc.vector.memset(zeros[:], 0.0)
             w_bank = work_banks.tile([P, 4 * P], F32, tag="bank")
@@ -281,7 +308,7 @@ def tile_normlocalattention_pa_t_kernel(tc, q_chunks, k_chunks, v_chunks, out):
                 score_bank(n)
             if n == 1 and not HEAD_SPLIT:
                 transpose_piece(True, 0, HALF, 2 * HALF, True)
-            if n == 3 and HEAD_SPLIT:
+            if n == Q47_AT and HEAD_SPLIT:
                 transpose_piece(False, 0, HALF, 2 * HALF, True)
             if n == 2 and not PACED:
                 regroup_values(0)
@@ -293,15 +320,23 @@ def tile_normlocalattention_pa_t_kernel(tc, q_chunks, k_chunks, v_chunks, out):
             if n - QUANT_LAG in unit_end:
                 quantise_scores(unit_end[n - QUANT_LAG])
             s, r = n // SLICE_BANKS + 1, n % SLICE_BANKS
-            if PACED and n % PACE_EVERY == PACE_AT and n // PACE_EVERY < SLICES * PASSES:
+            if PACED and n == VQ0_AT:
+                quantise_pass(0)
+                regroup_pass(1)
+            if PACED and n % PACE_EVERY == PACE_AT and 1 <= n // PACE_EVERY < SLICES * PASSES:
                 quantise_pass(n // PACE_EVERY)
                 if n // PACE_EVERY + 1 < SLICES * PASSES:
                     regroup_pass(n // PACE_EVERY + 1)
-            if s < SLICES:
+            if s < SLICES and FOUR_AT:
+                if r in FOUR_AT:
+                    piece = FOUR_AT.index(r)
+                    transpose_piece(piece % 2 == 0, s, piece // 2 * HALF, (piece // 2 + 1) * HALF, True)
+            elif s < SLICES:
                 if r == K_AT:
                     transpose_piece(True, s, 0, 2 * HALF, K_COPY_ON_VECTOR)
                 if r == Q_AT:
                     transpose_piece(False, s, 0, 2 * HALF, Q_COPY_ON_VECTOR)
+            if s < SLICES:
                 if r == REGROUP_AT and not PACED:
                     regroup_values(s)
                 if r == VQUANT_AT and not PACED:

@@ -31,12 +31,12 @@ STORE_LAG = 14
 K_AT, Q_AT, REGROUP_AT, VQUANT_AT = [6, 10, 8, 12]
 VECTOR_BANKS = [0]
 VECTOR_PERIOD = 4
-SCALAR_STORES = 3
+SCALAR_STORES = 4
 K_COPY_ON_VECTOR = True
 Q_COPY_ON_VECTOR = True
 WARM = 3
 SCALAR_QUEUE = False
-EXTRA_VECTOR = ()
+EXTRA_VECTOR = (61,)
 V0_LAST = False
 Q47_AT = 3
 VQ0_AT = 2

from contextlib import ExitStack

import concourse.mybir as mybir
from concourse.masks import make_identity

BF16 = mybir.dt.bfloat16
F32 = mybir.dt.float32
U32 = mybir.dt.uint32
U8 = mybir.dt.uint8
FP8X4 = mybir.dt.float8_e4m3fn_x4
RELU = mybir.ActivationFunctionType.Relu

P = 128
PACK = 4
SLICES = 4
CHUNK = 1024
HEAD = 128
PASSES = CHUNK // (P * PACK)
Q_TILES = CHUNK // P
BANKS = SLICES * Q_TILES * PASSES
SLICE_BANKS = Q_TILES * PASSES
HALF = 4

SLICE_GROUPS = ((4, 4), (4, 4), (4, 4), (4, 2, 2))
MAX_GROUP = 4
WORK_BANKS = 7
OUT_BANKS = 1
QUANT_LAG = 3
ATTEND_LAG = 12
STORE_LAG = 14
K_AT, Q_AT, REGROUP_AT, VQUANT_AT = [6, 10, 8, 12]
VECTOR_BANKS = [0]
VECTOR_PERIOD = 4
SCALAR_STORES = 4
K_COPY_ON_VECTOR = True
Q_COPY_ON_VECTOR = True
WARM = 3
SCALAR_QUEUE = False
EXTRA_VECTOR = (61,)
V0_LAST = False
Q47_AT = 3
VQ0_AT = 2
TAIL_WORK = 3
FOUR_AT = ()
TWO_QUEUES = False
WARM_EARLY = False
HEAD_SPLIT = True
PACED = True
PACE_EVERY, PACE_AT = (8, 2)
V_BUFS = 1
EXTRA_AT = ()
SHARE = 1
REGROUP_ON_GPSIMD = True

FLOPS = 2 * 2 * SLICES * CHUNK * CHUNK * HEAD


def tile_normlocalattention_pa_t_kernel(tc, q_chunks, k_chunks, v_chunks, out):
    nc = tc.nc

    q_dram = q_chunks.rearrange("n g (p t) d -> (n g) p t d", t=Q_TILES)
    k_dram = k_chunks.rearrange("n g (c p j) d -> (n g) p c j d", c=PASSES, j=PACK)
    v_dram = v_chunks.rearrange("n g (c p j) d -> (n g) p c j d", c=PASSES, j=PACK)
    out_dram = out.rearrange("n g (p t) d -> (n g) p t d", t=Q_TILES)

    groups, units, banks = [], [], []
    unit_end, group_end = {}, {}
    for s in range(SLICES):
        first = 0
        for size in SLICE_GROUPS[s]:
            g = len(groups)
            groups.append((s, first, size))
            first += size
            for c in range(PASSES):
                u = len(units)
                units.append((g, c))
                for i in range(size):
                    banks.append((u, i))
                unit_end[len(banks) - 1] = u
            group_end[len(banks) - 1] = g
    assert len(banks) == BANKS

    with ExitStack() as ctx:
        const = ctx.enter_context(tc.tile_pool(name="const", bufs=1))
        per_slice = ctx.enter_context(tc.tile_pool(name="per_slice", bufs=SLICES))
        per_unit = ctx.enter_context(tc.tile_pool(name="per_unit", bufs=8))
        one_pass = ctx.enter_context(tc.tile_pool(name="one_pass", bufs=V_BUFS))
        work_banks = ctx.enter_context(tc.psum_pool(name="work_banks", bufs=WORK_BANKS))
        out_banks = ctx.enter_context(tc.psum_pool(name="out_banks", bufs=OUT_BANKS))
        ctx.enter_context(tc.manual_schedule())

        if WARM and WARM_EARLY:
            zeros = const.tile([P, P], BF16)
            nc.gpsimd.memset(zeros[:], 0.0)
            w_bank = work_banks.tile([P, P], F32, tag="bank")
            for i in range(WARM):
                nc.tensor.matmul(out=w_bank[:], lhsT=zeros[:], rhs=zeros[:], start=True, stop=True)

        identity = const.tile([P, P], BF16)
        make_identity(nc, identity[:])

        k_in, q_in, v_in = [], [], []
        for s in range(SLICES):
            k_rows = per_slice.tile([P, PASSES, PACK, HEAD], BF16)
            q_rows = per_slice.tile([P, Q_TILES, HEAD], BF16)
            v_rows = per_slice.tile([P, PASSES, PACK, HEAD], BF16)
            if s == 0 and HEAD_SPLIT:
                second = nc.scalar if TWO_QUEUES else nc.sync
                second.dma_start(out=q_rows[:, 0:2, :], in_=q_dram[s, :, 0:2, :])
                nc.sync.dma_start(out=k_rows[:, 0, :, :], in_=k_dram[s, :, 0, :, :])
                second.dma_start(out=q_rows[:, 2:HALF, :], in_=q_dram[s, :, 2:HALF, :])
                nc.sync.dma_start(out=k_rows[:, 1, :, :], in_=k_dram[s, :, 1, :, :])
                if V0_LAST:
                    nc.sync.dma_start(out=q_rows[:, HALF:Q_TILES, :], in_=q_dram[s, :, HALF:Q_TILES, :])
                    nc.sync.dma_start(out=v_rows[:], in_=v_dram[s, :, :, :, :])
                else:
                    nc.sync.dma_start(out=v_rows[:], in_=v_dram[s, :, :, :, :])
                    nc.sync.dma_start(out=q_rows[:, HALF:Q_TILES, :], in_=q_dram[s, :, HALF:Q_TILES, :])
            elif s == 0:
                nc.sync.dma_start(out=k_rows[:, 0, :, :], in_=k_dram[s, :, 0, :, :])
                nc.sync.dma_start(out=q_rows[:, 0:HALF, :], in_=q_dram[s, :, 0:HALF, :])
                nc.sync.dma_start(out=k_rows[:, 1, :, :], in_=k_dram[s, :, 1, :, :])
                nc.sync.dma_start(out=v_rows[:], in_=v_dram[s, :, :, :, :])
                nc.sync.dma_start(out=q_rows[:, HALF:Q_TILES, :], in_=q_dram[s, :, HALF:Q_TILES, :])
            else:
                nc.sync.dma_start(out=k_rows[:], in_=k_dram[s, :, :, :, :])
                nc.sync.dma_start(out=q_rows[:], in_=q_dram[s, :, :, :])
                nc.sync.dma_start(out=v_rows[:], in_=v_dram[s, :, :, :, :])
            k_in.append(k_rows)
            q_in.append(q_rows)
            v_in.append(v_rows)

        k_t, q_t, v_grouped, v_codes, v_scales = [], [], [], [], []
        for s in range(SLICES):
            k_cols = per_slice.tile([P, PASSES * PACK, P], BF16)
            q_cols = per_slice.tile([P, Q_TILES, P], BF16)
            v_quads = per_slice.tile([P, PASSES, HEAD, PACK], BF16, align_bytes=64)
            v_words = per_slice.tile([P, PASSES, HEAD], U32, align_bytes=64)
            v_plane = per_slice.tile([P, PASSES, HEAD], U8, align_bytes=64)
            k_t.append(k_cols)
            q_t.append(q_cols)
            v_grouped.append(v_quads)
            v_codes.append(v_words)
            v_scales.append(v_plane)

        def transpose_piece(is_k, s, lo, hi, on_vector):
            t_bank = work_banks.tile([P, hi - lo, P], BF16, tag="bank")
            if is_k:
                rows, cols = k_in[s][:].rearrange("p c j d -> p (c j) d"), k_t[s]
            else:
                rows, cols = q_in[s][:], q_t[s]
            for i in range(lo, hi):
                nc.tensor.transpose(out=t_bank[:, i - lo, :], in_=rows[:, i, :], identity=identity[:])
            if on_vector:
                nc.vector.tensor_copy(out=cols[:, lo:hi, :], in_=t_bank[:])
            else:
                nc.scalar.copy(out=cols[:, lo:hi, :], in_=t_bank[:])

        def regroup_values(s):
            for c in range(PASSES):
                if REGROUP_ON_GPSIMD:
                    nc.gpsimd.tensor_scalar(
                        out=v_grouped[s][:, c, :, :],
                        in0=v_in[s][:, c, :, :].rearrange("p j d -> p d j"),
                        scalar1=1.0,
                        scalar2=0.0,
                        op0=mybir.AluOpType.mult,
                        op1=mybir.AluOpType.add,
                    )
                    continue
                nc.vector.tensor_copy(
                    out=v_grouped[s][:, c, :, :].rearrange("p (a i) j -> p a j i", i=4),
                    in_=v_in[s][:, c, :, :].rearrange("p j (a i) -> p a j i", i=4),
                )

        def quantise_values(s):
            nc.vector.quantize_mx(
                out=v_codes[s][:].rearrange("p c d -> p (c d)").bitcast(FP8X4),
                scales=v_scales[s][:].rearrange("p c d -> p (c d)"),
                in_=v_grouped[s][:].rearrange("p c d j -> p (c d j)"),
            )

        v_pass = {}

        def regroup_pass(w):
            s, c = w // PASSES, w % PASSES
            quads_v = one_pass.tile([P, HEAD, PACK], BF16, align_bytes=64)
            v_pass[w] = quads_v
            nc.gpsimd.tensor_scalar(
                out=quads_v[:],
                in0=v_in[s][:, c, :, :].rearrange("p j d -> p d j"),
                scalar1=1.0,
                scalar2=0.0,
                op0=mybir.AluOpType.mult,
                op1=mybir.AluOpType.add,
            )

        def quantise_pass(w):
            s, c = w // PASSES, w % PASSES
            nc.vector.quantize_mx(
                out=v_codes[s][:, c, :].bitcast(FP8X4),
                scales=v_scales[s][:, c, :],
                in_=v_pass[w][:].rearrange("p d j -> p (d j)"),
            )

        p_grouped, p_codes, p_scales = {}, {}, {}
        s_banks = {}

        def score_bank(n):
            u, i = banks[n]
            g, c = units[u]
            s, first, size = groups[g]
            t = first + i
            if i == 0:
                quads = per_unit.tile([P, MAX_GROUP, P, PACK], BF16, align_bytes=64)
                words = per_unit.tile([P, MAX_GROUP * P], U32, align_bytes=64)
                plane = per_unit.tile([P, MAX_GROUP * P], U8, align_bytes=64)
                p_grouped[u], p_codes[u], p_scales[u] = quads, words, plane
            if i % SHARE == 0:
                for e in range(SHARE):
                    s_bank = work_banks.tile([P, PACK, P], F32, tag="bank")
                    s_banks[n + e] = s_bank
                if n % 8 in EXTRA_AT:
                    nc.tensor.matmul(
                        out=s_banks[n][:, 0, :],
                        lhsT=k_t[s][:, c * PACK, :],
                        rhs=q_t[s][:, t, :],
                        start=True,
                        stop=True,
                    )
                for j in range(PACK):
                    for e in range(SHARE):
                        nc.tensor.matmul(
                            out=s_banks[n + e][:, j, :],
                            lhsT=k_t[s][:, c * PACK + j, :],
                            rhs=q_t[s][:, t + e, :],
                            start=True,
                            stop=True,
                        )
            by_query = s_banks[n][:].rearrange("p j q -> p q j")
            if n % VECTOR_PERIOD in VECTOR_BANKS or n in EXTRA_VECTOR:
                nc.vector.tensor_scalar_max(out=p_grouped[u][:, i, :, :], in0=by_query, scalar1=0.0)
            else:
                nc.scalar.activation(out=p_grouped[u][:, i, :, :], in_=by_query, func=RELU)

        def quantise_scores(u):
            size = groups[units[u][0]][2]
            nc.vector.quantize_mx(
                out=p_codes[u][:, 0 : size * P].bitcast(FP8X4),
                scales=p_scales[u][:, 0 : size * P],
                in_=p_grouped[u][:, 0:size, :, :].rearrange("p i q j -> p (i q j)"),
            )

        o_banks = {}

        def attend(g):
            s, first, size = groups[g]
            if g >= len(groups) - TAIL_WORK:
                o_bank = work_banks.tile([P, MAX_GROUP, HEAD], F32, tag="bank")
            else:
                o_bank = out_banks.tile([P, MAX_GROUP, HEAD], F32, tag="out")
            o_banks[g] = o_bank
            for i in range(size):
                queries = slice(i * P, (i + 1) * P)
                for c in range(PASSES):
                    u = g * PASSES + c
                    nc.tensor.matmul_mx(
                        out=o_bank[:, i, :],
                        lhsT=p_codes[u][:, queries].bitcast(FP8X4),
                        lhsT_scale=p_scales[u][:, queries],
                        rhs=v_codes[s][:, c, :].bitcast(FP8X4),
                        rhs_scale=v_scales[s][:, c, :],
                        start=(c == 0),
                        stop=(c == PASSES - 1),
                    )

        def store(g):
            s, first, size = groups[g]
            o_rows = per_unit.tile([P, MAX_GROUP, HEAD], F32)
            if g >= len(groups) - SCALAR_STORES:
                nc.scalar.copy(out=o_rows[:, 0:size, :], in_=o_banks[g][:, 0:size, :])
            else:
                nc.vector.tensor_copy(out=o_rows[:, 0:size, :], in_=o_banks[g][:, 0:size, :])
            if g >= len(groups) - SCALAR_STORES and SCALAR_QUEUE:
                nc.scalar.dma_start(out=out_dram[s, :, first : first + size, :], in_=o_rows[:, 0:size, :])
            else:
                nc.sync.dma_start(out=out_dram[s, :, first : first + size, :], in_=o_rows[:, 0:size, :])

        if WARM and not WARM_EARLY:
            zeros = const.tile([P, 4 * P], BF16)
            nc.vector.memset(zeros[:], 0.0)
            w_bank = work_banks.tile([P, 4 * P], F32, tag="bank")
            for i in range(WARM):
                nc.tensor.matmul(out=w_bank[:], lhsT=zeros[:, 0:P], rhs=zeros[:], start=True, stop=True)
        if PACED:
            regroup_pass(0)
        if HEAD_SPLIT:
            transpose_piece(False, 0, 0, 2, True)
            transpose_piece(True, 0, 0, HALF, True)
            transpose_piece(False, 0, 2, HALF, False)
            transpose_piece(True, 0, HALF, 2 * HALF, True)
        else:
            transpose_piece(True, 0, 0, HALF, True)
            transpose_piece(False, 0, 0, HALF, False)

        for n in range(BANKS + STORE_LAG + 1):
            if n < BANKS:
                score_bank(n)
            if n == 1 and not HEAD_SPLIT:
                transpose_piece(True, 0, HALF, 2 * HALF, True)
            if n == Q47_AT and HEAD_SPLIT:
                transpose_piece(False, 0, HALF, 2 * HALF, True)
            if n == 2 and not PACED:
                regroup_values(0)
            if n == 4:
                if not HEAD_SPLIT:
                    transpose_piece(False, 0, HALF, 2 * HALF, False)
                if not PACED:
                    quantise_values(0)
            if n - QUANT_LAG in unit_end:
                quantise_scores(unit_end[n - QUANT_LAG])
            s, r = n // SLICE_BANKS + 1, n % SLICE_BANKS
            if PACED and n == VQ0_AT:
                quantise_pass(0)
                regroup_pass(1)
            if PACED and n % PACE_EVERY == PACE_AT and 1 <= n // PACE_EVERY < SLICES * PASSES:
                quantise_pass(n // PACE_EVERY)
                if n // PACE_EVERY + 1 < SLICES * PASSES:
                    regroup_pass(n // PACE_EVERY + 1)
            if s < SLICES and FOUR_AT:
                if r in FOUR_AT:
                    piece = FOUR_AT.index(r)
                    transpose_piece(piece % 2 == 0, s, piece // 2 * HALF, (piece // 2 + 1) * HALF, True)
            elif s < SLICES:
                if r == K_AT:
                    transpose_piece(True, s, 0, 2 * HALF, K_COPY_ON_VECTOR)
                if r == Q_AT:
                    transpose_piece(False, s, 0, 2 * HALF, Q_COPY_ON_VECTOR)
            if s < SLICES:
                if r == REGROUP_AT and not PACED:
                    regroup_values(s)
                if r == VQUANT_AT and not PACED:
                    quantise_values(s)
            if n - ATTEND_LAG in group_end:
                attend(group_end[n - ATTEND_LAG])
            if n - STORE_LAG in group_end:
                store(group_end[n - STORE_LAG])
